import numpy as np
import ml_dtypes


def mxq(x, axis, fmt="e4m3"):
    dtype, down = {"e4m3": (ml_dtypes.float8_e4m3fn, 7), "e5m2": (ml_dtypes.float8_e5m2, 14)}[fmt]
    v = np.moveaxis(np.asarray(x, np.float32).astype(ml_dtypes.bfloat16).astype(np.float64), axis, -1)
    blocks = v.reshape(v.shape[:-1] + (-1, 32))
    amax = np.abs(blocks).max(-1, keepdims=True)
    byte = np.maximum(np.where(amax > 0, np.frexp(amax)[1] - 1 + 127, 0) - down, 1)
    scale = np.exp2(byte - 127.0)
    codes = (blocks / scale).astype(np.float32).astype(dtype).astype(np.float64)
    return np.moveaxis((codes * scale).reshape(v.shape), -1, axis)


WIDE = False


def mx_kscale(k):
    if not WIDE:
        return np.ones(k)
    levels = np.array([10, -10, 5, -5, 0])
    if k % 512:
        return np.exp2(np.random.permutation(np.resize(levels, k // 32))).repeat(32)
    a = np.empty((k // 512, 16))
    for p in range(k // 512):
        a[p, :8] = np.random.permutation(np.resize(levels, 8))
        for g in range(8):
            far = levels[np.abs(levels - a[p, g]) >= 10]
            a[p, g + 8] = far[np.random.randint(len(far))]
    return np.exp2(a.ravel()).repeat(32)


BF16 = ml_dtypes.bfloat16


def bf(x):
    return np.asarray(x, np.float32).astype(BF16)


def f64(x):
    return np.asarray(x).astype(np.float64)


B, S, D, H, DH = 1, 1024, 1024, 8, 128
E = H * DH
EPS = 1e-12


def rotate_half(t):
    t1, t2 = np.split(t, 2, axis=-1)
    return np.concatenate((-t2, t1), axis=-1)


def apply_rotary(pos, t):
    return t * np.cos(pos) + rotate_half(t) * np.sin(pos)


def setup_inputs():
    s = mx_kscale(D)
    ang = np.random.uniform(-np.pi, np.pi, (S, DH // 2))
    col = np.concatenate((np.full(E, np.sqrt(3.0 / DH)), np.full(E, np.sqrt(3.0 / DH)), np.ones(E)))
    return {"x": bf(np.random.standard_normal((B, S, D))),
            "rotary_emb": bf(np.concatenate((ang, ang), axis=-1)),
            "gamma": bf((1.0 + 0.1 * np.random.standard_normal(D)) * s),
            "w_qkv": bf(np.random.standard_normal((D, 3 * E)) * col / np.sqrt(D) / s[:, None])}


def reference(x, rotary_emb, gamma, w_qkv):
    x, pos = f64(x), f64(rotary_emb)
    l2 = np.sqrt((x * x).sum(-1, keepdims=True))
    xn = x / np.maximum(l2, EPS) * np.sqrt(D) * f64(gamma)
    qkv = mxq(xn, 2, "e4m3") @ mxq(f64(w_qkv), 0, "e4m3")
    qkv = qkv.reshape(B, S, 3, H, DH).transpose(2, 0, 3, 1, 4)
    q, k, v = qkv[0], qkv[1], qkv[2]
    q = apply_rotary(pos, q)
    k = apply_rotary(pos, k)
    q = q * np.sqrt(DH)
    return q, k, v

@@ -1,0 +1,211 @@
+import math
+from contextlib import ExitStack
+
+import concourse.mybir as mybir
+from concourse.masks import make_identity
+
+FP8X4 = mybir.dt.float8_e4m3fn_x4
+BF16 = mybir.dt.bfloat16
+F32 = mybir.dt.float32
+U32 = mybir.dt.uint32
+U8 = mybir.dt.uint8
+ACT = mybir.ActivationFunctionType
+ALU = mybir.AluOpType
+
+P = 128
+SEQ = 1024
+DIM = 1024
+HEADS = 8
+DH = 128
+HALF = DH // 2
+EPS = 1e-12
+
+PACK = 4
+K_PASS = P * PACK
+PASSES = DIM // K_PASS
+PAIRS = PACK // 2
+ROW_TILES = SEQ // P
+N_COLS = 512
+GROUP_HEADS = N_COLS // DH
+T_RUN = 4
+T_RUN_LAST = 2
+
+GROUPS = ((0, 0), (0, 1), (2, 0), (1, 0), (2, 1), (1, 1))
+
+FLOPS = 2 * SEQ * DIM * 3 * HEADS * DH
+
+
+def tile_ringattention_pa_kernel(tc, x, rotary_emb, gamma, w_qkv, out_q, out_k, out_v):
+    nc = tc.nc
+    outs = (out_q, out_k, out_v)
+    with ExitStack() as ctx:
+        keep = ctx.enter_context(tc.tile_pool(name="keep", bufs=1))
+        squares = ctx.enter_context(tc.tile_pool(name="squares", bufs=2))
+        normed = ctx.enter_context(tc.tile_pool(name="normed", bufs=3))
+        w_in = ctx.enter_context(tc.tile_pool(name="w_in", bufs=len(GROUPS) - 1))
+        w_words = ctx.enter_context(tc.tile_pool(name="w_words", bufs=2))
+        w_mx = ctx.enter_context(tc.tile_pool(name="w_mx", bufs=3))
+        products = ctx.enter_context(tc.tile_pool(name="products", bufs=3))
+        results = ctx.enter_context(tc.tile_pool(name="results", bufs=3))
+        results_v = ctx.enter_context(tc.tile_pool(name="results_v", bufs=2))
+        psum_v = ctx.enter_context(tc.psum_pool(name="psum_v", bufs=5))
+        psum_s = ctx.enter_context(tc.psum_pool(name="psum_s", bufs=3))
+
+        angles = keep.tile([P, ROW_TILES, DH], BF16)
+        nc.sync.dma_start(out=angles[:], in_=rotary_emb.rearrange("(p t) d -> p t d", t=ROW_TILES))
+        gamma_row = keep.tile([P, DIM], BF16)
+        nc.vector.memset(gamma_row[:], 0.0)
+        nc.sync.dma_start(out=gamma_row[0:1, :], in_=gamma.rearrange("(o k) -> o k", o=1))
+        x_rows = keep.tile([P, ROW_TILES, DIM], BF16)
+        x_view = x[0].rearrange("(p t) k -> p t k", t=ROW_TILES)
+        w_view = w_qkv.rearrange("(g p u) n -> g p u n", p=P, u=PACK)
+        w_raw = {}
+
+        def load_x(t):
+            nc.sync.dma_start(out=x_rows[:, t : t + 2, :], in_=x_view[:, t : t + 2, :])
+
+        def load_w(section, half):
+            first = (section * 2 + half) * N_COLS
+            w_raw[(section, half)] = w_in.tile([P, PASSES, PACK, N_COLS], BF16, name="w_raw")
+            for g in range(PASSES):
+                nc.sync.dma_start(out=w_raw[(section, half)][:, g], in_=w_view[g, :, :, first : first + N_COLS])
+
+        load_x(0)
+        load_w(*GROUPS[0])
+        for t in range(2, ROW_TILES, 2):
+            load_x(t)
+        for section, half in GROUPS[1:]:
+            load_w(section, half)
+
+        ident = keep.tile([P, P], F32)
+        make_identity(nc, ident[:])
+        ones = keep.tile([P, P], BF16)
+        nc.vector.memset(ones[:], 1.0)
+        minus_half = keep.tile([P, ROW_TILES], F32)
+        nc.gpsimd.memset(minus_half[:], -0.5)
+
+        table_k = keep.tile([P, ROW_TILES, 2, DH], F32)
+        table_q = keep.tile([P, ROW_TILES, 2, DH], F32)
+        sin_half = keep.tile([P, ROW_TILES, DH], F32)
+        nc.scalar.activation(out=sin_half[:], in_=angles[:], func=ACT.Sin, scale=0.5)
+        nc.scalar.activation(out=table_k[:, :, 1, 0:HALF], in_=angles[:, :, HALF:DH], func=ACT.Sin)
+        nc.scalar.activation(out=table_k[:, :, 1, HALF:DH], in_=angles[:, :, 0:HALF], func=ACT.Sin, scale=-1.0)
+        nc.vector.tensor_tensor(out=sin_half[:], in0=sin_half[:], in1=sin_half[:], op=ALU.mult)
+        nc.vector.tensor_scalar(
+            out=table_k[:, :, 0, :], in0=sin_half[:], scalar1=-2.0, scalar2=1.0, op0=ALU.mult, op1=ALU.add
+        )
+        tables = (table_q, table_k)
+
+        gamma_all = keep.tile([P, DIM], BF16)
+        for n in range(0, DIM, N_COLS):
+            spread = psum_v.tile([P, N_COLS], F32, tag="bank")
+            nc.tensor.matmul(out=spread[:], lhsT=ones[:], rhs=gamma_row[:, n : n + N_COLS], start=True, stop=True)
+            nc.vector.tensor_copy(out=gamma_all[:, n : n + N_COLS], in_=spread[:])
+
+        x_codes = keep.tile([P, ROW_TILES, PASSES, P], U32, align_bytes=64)
+        x_scales = keep.tile([P, ROW_TILES, PASSES, P], U8, align_bytes=64)
+        mean_sq = keep.tile([P, ROW_TILES], F32)
+        floored = keep.tile([P, ROW_TILES], F32)
+        inv_rms = keep.tile([P, ROW_TILES], F32)
+        for t in range(ROW_TILES):
+            sq = squares.tile([P, DIM], BF16)
+            nc.scalar.activation(
+                out=sq[:], in_=x_rows[:, t, :], func=ACT.Square, scale=1.0 / math.sqrt(DIM),
+                accum_out=mean_sq[:, t : t + 1],
+            )
+            nc.gpsimd.tensor_scalar(
+                out=floored[:, t : t + 1], in0=mean_sq[:, t : t + 1], scalar1=EPS * EPS / DIM, scalar2=None,
+                op0=ALU.max,
+            )
+            nc.gpsimd.tensor_tensor(
+                out=inv_rms[:, t : t + 1], in0=floored[:, t : t + 1], in1=minus_half[:, t : t + 1], op=ALU.pow
+            )
+            xn = normed.tile([P, DIM], BF16)
+            nc.vector.scalar_tensor_tensor(
+                out=xn[:], in0=x_rows[:, t, :], scalar=inv_rms[:, t : t + 1], in1=gamma_all[:],
+                op0=ALU.mult, op1=ALU.mult,
+            )
+            pairs = xn[:].bitcast(F32)
+            xn_t = psum_s.tile([P, PASSES, PAIRS, P], F32, tag="bank")
+            for g in range(PASSES):
+                for h in range(PAIRS):
+                    first = g * P * PAIRS + h
+                    nc.tensor.transpose(xn_t[:, g, h, :], pairs[:, first : (g + 1) * P * PAIRS : PAIRS], ident[:])
+            xn_words = normed.tile([P, PASSES, P, PAIRS], F32, align_bytes=64)
+            nc.scalar.copy(out=xn_words[:], in_=xn_t[:].rearrange("p g h r -> p g r h"))
+            nc.vector.quantize_mx(
+                out=x_codes[:, t].rearrange("p g r -> p (g r)").bitcast(FP8X4),
+                scales=x_scales[:, t].rearrange("p g r -> p (g r)"),
+                in_=xn_words[:].rearrange("p g r h -> p (g r h)").bitcast(BF16),
+            )
+
+        nc.vector.tensor_scalar_mul(out=table_q[:], in0=table_k[:], scalar1=math.sqrt(DH))
+
+        def quantise_weights(index):
+            codes = w_mx.tile([P, PASSES, N_COLS], U32, align_bytes=64, name="w_codes")
+            scales = w_mx.tile([P, PASSES, N_COLS], U8, align_bytes=64, name="w_scales")
+            grouped = w_words.tile([P, PASSES, N_COLS, PACK], BF16, align_bytes=64, name="grouped")
+            regroup = nc.vector.tensor_copy if index == 0 else nc.scalar.copy
+            for g in range(PASSES):
+                regroup(
+                    out=grouped[:, g].rearrange("p (c i) u -> p c u i", i=4),
+                    in_=w_raw[GROUPS[index]][:, g].rearrange("p u (c i) -> p c u i", i=4),
+                )
+            nc.vector.quantize_mx(
+                out=codes[:].rearrange("p g n -> p (g n)").bitcast(FP8X4),
+                scales=scales[:].rearrange("p g n -> p (g n)"),
+                in_=grouped[:].rearrange("p g n u -> p (g n u)"),
+            )
+            return codes, scales
+
+        ahead = quantise_weights(0)
+        for index, (section, half) in enumerate(GROUPS):
+            w_codes, w_scales = ahead
+            if index + 1 < len(GROUPS):
+                ahead = quantise_weights(index + 1)
+            out_view = outs[section][0].rearrange("h (p t) d -> p h t d", t=ROW_TILES)
+            first_head = half * GROUP_HEADS
+            last_group = index == len(GROUPS) - 1
+            t_run = T_RUN_LAST if last_group else T_RUN
+            for t0 in range(0, ROW_TILES, t_run):
+                result = (results if section < 2 else results_v).tile([P, GROUP_HEADS, t_run, DH], F32, name="result")
+                if section < 2:
+                    product = products.tile([P, t_run, 2, GROUP_HEADS, DH], F32)
+                for j in range(t_run):
+                    t = t0 + j
+                    acc = (psum_v if section < 2 else psum_s).tile([P, N_COLS], F32, tag="bank", name="acc")
+                    for g in range(PASSES):
+                        nc.tensor.matmul_mx(
+                            out=acc[:],
+                            lhsT=x_codes[:, t, g, :].bitcast(FP8X4),
+                            lhsT_scale=x_scales[:, t, g, :],
+                            rhs=w_codes[:, g, :].bitcast(FP8X4),
+                            rhs_scale=w_scales[:, g, :],
+                            start=(g == 0),
+                            stop=(g == PASSES - 1),
+                        )
+                    by_head = acc[:].rearrange("p (h d) -> p h d", h=GROUP_HEADS)
+                    if section < 2:
+                        both = [P, 2, GROUP_HEADS, DH]
+                        nc.vector.tensor_tensor(
+                            out=product[:, j],
+                            in0=by_head.unsqueeze(1).to_broadcast(both),
+                            in1=tables[section][:, t].unsqueeze(2).to_broadcast(both),
+                            op=ALU.mult,
+                        )
+                    else:
+                        nc.scalar.copy(out=result[:, :, j, :], in_=by_head)
+                if section < 2:
+                    for lo in (0, HALF):
+                        partner = HALF - lo
+                        adder = nc.vector if last_group and lo == HALF else nc.gpsimd
+                        adder.tensor_tensor(
+                            out=result[:, :, :, lo : lo + HALF].rearrange("p h t d -> p t h d"),
+                            in0=product[:, :, 0, :, lo : lo + HALF],
+                            in1=product[:, :, 1, :, partner : partner + HALF],
+                            op=ALU.add,
+                        )
+                store_queue = nc.sync if section < 2 else nc.scalar
+                store_queue.dma_start(
+                    out=out_view[:, first_head : first_head + GROUP_HEADS, t0 : t0 + t_run, :], in_=result[:]
+                )

@@ -28,9 +28,12 @@ ROW_TILES = SEQ // P
 N_COLS = 512
 GROUP_HEADS = N_COLS // DH
 T_RUN = 4
+ADD_RUN = 2
 T_RUN_LAST = 2
 
-GROUPS = ((0, 0), (0, 1), (2, 0), (1, 0), (2, 1), (1, 1))
+GROUPS = ((1, 0), (1, 1), (0, 0), (2, 0), (0, 1), (2, 1))
+
+LAST_ROTARY = 4
 
 FLOPS = 2 * SEQ * DIM * 3 * HEADS * DH
 
@@ -43,13 +46,13 @@ def tile_ringattention_pa_kernel(tc, x, rotary_emb, gamma, w_qkv, out_q, out_k, 
         squares = ctx.enter_context(tc.tile_pool(name="squares", bufs=2))
         normed = ctx.enter_context(tc.tile_pool(name="normed", bufs=3))
         w_in = ctx.enter_context(tc.tile_pool(name="w_in", bufs=len(GROUPS) - 1))
-        w_words = ctx.enter_context(tc.tile_pool(name="w_words", bufs=2))
-        w_mx = ctx.enter_context(tc.tile_pool(name="w_mx", bufs=3))
-        products = ctx.enter_context(tc.tile_pool(name="products", bufs=3))
-        results = ctx.enter_context(tc.tile_pool(name="results", bufs=3))
+        w_words = ctx.enter_context(tc.tile_pool(name="w_words", bufs=3))
+        w_mx = ctx.enter_context(tc.tile_pool(name="w_mx", bufs=4))
+        products = ctx.enter_context(tc.tile_pool(name="products", bufs=4))
+        results = ctx.enter_context(tc.tile_pool(name="results", bufs=4))
         results_v = ctx.enter_context(tc.tile_pool(name="results_v", bufs=2))
-        psum_v = ctx.enter_context(tc.psum_pool(name="psum_v", bufs=5))
-        psum_s = ctx.enter_context(tc.psum_pool(name="psum_s", bufs=3))
+        psum_v = ctx.enter_context(tc.psum_pool(name="psum_v", bufs=4))
+        psum_s = ctx.enter_context(tc.psum_pool(name="psum_s", bufs=4))
 
         angles = keep.tile([P, ROW_TILES, DH], BF16)
         nc.sync.dma_start(out=angles[:], in_=rotary_emb.rearrange("(p t) d -> p t d", t=ROW_TILES))
@@ -84,31 +87,44 @@ def tile_ringattention_pa_kernel(tc, x, rotary_emb, gamma, w_qkv, out_q, out_k, 
         minus_half = keep.tile([P, ROW_TILES], F32)
         nc.gpsimd.memset(minus_half[:], -0.5)
 
-        table_k = keep.tile([P, ROW_TILES, 2, DH], F32)
-        table_q = keep.tile([P, ROW_TILES, 2, DH], F32)
+        table_k = keep.tile([P, ROW_TILES, 2, 2, HALF], F32)
+        table_q = keep.tile([P, ROW_TILES, 2, 2, HALF], F32)
         sin_half = keep.tile([P, ROW_TILES, DH], F32)
         nc.scalar.activation(out=sin_half[:], in_=angles[:], func=ACT.Sin, scale=0.5)
-        nc.scalar.activation(out=table_k[:, :, 1, 0:HALF], in_=angles[:, :, HALF:DH], func=ACT.Sin)
-        nc.scalar.activation(out=table_k[:, :, 1, HALF:DH], in_=angles[:, :, 0:HALF], func=ACT.Sin, scale=-1.0)
         nc.vector.tensor_tensor(out=sin_half[:], in0=sin_half[:], in1=sin_half[:], op=ALU.mult)
-        nc.vector.tensor_scalar(
-            out=table_k[:, :, 0, :], in0=sin_half[:], scalar1=-2.0, scalar2=1.0, op0=ALU.mult, op1=ALU.add
-        )
+        for e in range(2):
+            nc.vector.tensor_scalar(
+                out=table_k[:, :, e, e, :], in0=sin_half[:, :, e * HALF : (e + 1) * HALF],
+                scalar1=-2.0, scalar2=1.0, op0=ALU.mult, op1=ALU.add,
+            )
+
+        def sine_tables():
+            nc.scalar.activation(out=table_k[:, :, 0, 1, :], in_=angles[:, :, 0:HALF], func=ACT.Sin, scale=-1.0)
+            nc.scalar.activation(out=table_k[:, :, 1, 0, :], in_=angles[:, :, HALF:DH], func=ACT.Sin)
+
+        def scaled_tables():
+            for e in range(2):
+                nc.gpsimd.tensor_scalar(
+                    out=table_q[:, :, e], in0=table_k[:, :, e], scalar1=math.sqrt(DH), scalar2=0.0,
+                    op0=ALU.mult, op1=ALU.add,
+                )
+
         tables = (table_q, table_k)
 
-        gamma_all = keep.tile([P, DIM], BF16)
+        gamma_all = []
         for n in range(0, DIM, N_COLS):
-            spread = psum_v.tile([P, N_COLS], F32, tag="bank")
+            spread = psum_s.tile([P, N_COLS], F32, tag="bank")
             nc.tensor.matmul(out=spread[:], lhsT=ones[:], rhs=gamma_row[:, n : n + N_COLS], start=True, stop=True)
-            nc.vector.tensor_copy(out=gamma_all[:, n : n + N_COLS], in_=spread[:])
+            gamma_all.append(spread)
 
         x_codes = keep.tile([P, ROW_TILES, PASSES, P], U32, align_bytes=64)
         x_scales = keep.tile([P, ROW_TILES, PASSES, P], U8, align_bytes=64)
         mean_sq = keep.tile([P, ROW_TILES], F32)
         floored = keep.tile([P, ROW_TILES], F32)
         inv_rms = keep.tile([P, ROW_TILES], F32)
-        for t in range(ROW_TILES):
-            sq = squares.tile([P, DIM], BF16)
+
+        def row_scale(t):
+            sq = squares.tile([P, DIM], BF16, name="sq")
             nc.scalar.activation(
                 out=sq[:], in_=x_rows[:, t, :], func=ACT.Square, scale=1.0 / math.sqrt(DIM),
                 accum_out=mean_sq[:, t : t + 1],
@@ -120,92 +136,148 @@ def tile_ringattention_pa_kernel(tc, x, rotary_emb, gamma, w_qkv, out_q, out_k, 
             nc.gpsimd.tensor_tensor(
                 out=inv_rms[:, t : t + 1], in0=floored[:, t : t + 1], in1=minus_half[:, t : t + 1], op=ALU.pow
             )
-            xn = normed.tile([P, DIM], BF16)
-            nc.vector.scalar_tensor_tensor(
-                out=xn[:], in0=x_rows[:, t, :], scalar=inv_rms[:, t : t + 1], in1=gamma_all[:],
-                op0=ALU.mult, op1=ALU.mult,
-            )
-            pairs = xn[:].bitcast(F32)
-            xn_t = psum_s.tile([P, PASSES, PAIRS, P], F32, tag="bank")
+
+        xn_of = {}
+        words_of = {}
+
+        def normalise(t):
+            xn = normed.tile([P, DIM], BF16, name="xn")
+            xn_of[t] = xn
+            for j, spread in enumerate(gamma_all):
+                cols = slice(j * N_COLS, (j + 1) * N_COLS)
+                nc.vector.scalar_tensor_tensor(
+                    out=xn[:, cols], in0=x_rows[:, t, cols], scalar=inv_rms[:, t : t + 1], in1=spread[:],
+                    op0=ALU.mult, op1=ALU.mult,
+                )
+
+        def turn(t):
+            pairs = xn_of[t][:].bitcast(F32)
+            xn_t = psum_s.tile([P, PASSES, PAIRS, P], F32, tag="bank", name="xn_t")
             for g in range(PASSES):
                 for h in range(PAIRS):
                     first = g * P * PAIRS + h
                     nc.tensor.transpose(xn_t[:, g, h, :], pairs[:, first : (g + 1) * P * PAIRS : PAIRS], ident[:])
-            xn_words = normed.tile([P, PASSES, P, PAIRS], F32, align_bytes=64)
+            xn_words = normed.tile([P, PASSES, P, PAIRS], F32, align_bytes=64, name="xn_words")
             nc.scalar.copy(out=xn_words[:], in_=xn_t[:].rearrange("p g h r -> p g r h"))
+            words_of[t] = xn_words
+
+        def quantise_rows(t):
             nc.vector.quantize_mx(
                 out=x_codes[:, t].rearrange("p g r -> p (g r)").bitcast(FP8X4),
                 scales=x_scales[:, t].rearrange("p g r -> p (g r)"),
-                in_=xn_words[:].rearrange("p g r h -> p (g r h)").bitcast(BF16),
+                in_=words_of[t][:].rearrange("p g r h -> p (g r h)").bitcast(BF16),
             )
 
-        nc.vector.tensor_scalar_mul(out=table_q[:], in0=table_k[:], scalar1=math.sqrt(DH))
+        grouped_of = {}
+        weights_of = {}
 
-        def quantise_weights(index):
-            codes = w_mx.tile([P, PASSES, N_COLS], U32, align_bytes=64, name="w_codes")
-            scales = w_mx.tile([P, PASSES, N_COLS], U8, align_bytes=64, name="w_scales")
+        def regroup_weights(index):
             grouped = w_words.tile([P, PASSES, N_COLS, PACK], BF16, align_bytes=64, name="grouped")
+            grouped_of[index] = grouped
             regroup = nc.vector.tensor_copy if index == 0 else nc.scalar.copy
             for g in range(PASSES):
                 regroup(
                     out=grouped[:, g].rearrange("p (c i) u -> p c u i", i=4),
                     in_=w_raw[GROUPS[index]][:, g].rearrange("p u (c i) -> p c u i", i=4),
                 )
+
+        def quantise_weights(index):
+            codes = w_mx.tile([P, PASSES, N_COLS], U32, align_bytes=64, name="w_codes")
+            scales = w_mx.tile([P, PASSES, N_COLS], U8, align_bytes=64, name="w_scales")
             nc.vector.quantize_mx(
                 out=codes[:].rearrange("p g n -> p (g n)").bitcast(FP8X4),
                 scales=scales[:].rearrange("p g n -> p (g n)"),
-                in_=grouped[:].rearrange("p g n u -> p (g n u)"),
+                in_=grouped_of[index][:].rearrange("p g n u -> p (g n u)"),
             )
-            return codes, scales
+            weights_of[index] = (codes, scales)
 
-        ahead = quantise_weights(0)
-        for index, (section, half) in enumerate(GROUPS):
-            w_codes, w_scales = ahead
-            if index + 1 < len(GROUPS):
-                ahead = quantise_weights(index + 1)
-            out_view = outs[section][0].rearrange("h (p t) d -> p h t d", t=ROW_TILES)
-            first_head = half * GROUP_HEADS
-            last_group = index == len(GROUPS) - 1
+        results_of = {}
+        products_of = {}
+
+        def bank(index, t):
+            w_codes, w_scales = weights_of[index]
+            section, half = GROUPS[index]
+            last_group = index == LAST_ROTARY
             t_run = T_RUN_LAST if last_group else T_RUN
-            for t0 in range(0, ROW_TILES, t_run):
-                result = (results if section < 2 else results_v).tile([P, GROUP_HEADS, t_run, DH], F32, name="result")
-                if section < 2:
-                    product = products.tile([P, t_run, 2, GROUP_HEADS, DH], F32)
-                for j in range(t_run):
-                    t = t0 + j
-                    acc = (psum_v if section < 2 else psum_s).tile([P, N_COLS], F32, tag="bank", name="acc")
-                    for g in range(PASSES):
-                        nc.tensor.matmul_mx(
-                            out=acc[:],
-                            lhsT=x_codes[:, t, g, :].bitcast(FP8X4),
-                            lhsT_scale=x_scales[:, t, g, :],
-                            rhs=w_codes[:, g, :].bitcast(FP8X4),
-                            rhs_scale=w_scales[:, g, :],
-                            start=(g == 0),
-                            stop=(g == PASSES - 1),
-                        )
-                    by_head = acc[:].rearrange("p (h d) -> p h d", h=GROUP_HEADS)
-                    if section < 2:
-                        both = [P, 2, GROUP_HEADS, DH]
-                        nc.vector.tensor_tensor(
-                            out=product[:, j],
-                            in0=by_head.unsqueeze(1).to_broadcast(both),
-                            in1=tables[section][:, t].unsqueeze(2).to_broadcast(both),
-                            op=ALU.mult,
-                        )
-                    else:
-                        nc.scalar.copy(out=result[:, :, j, :], in_=by_head)
-                if section < 2:
-                    for lo in (0, HALF):
-                        partner = HALF - lo
-                        adder = nc.vector if last_group and lo == HALF else nc.gpsimd
+            j = t % t_run
+            if j == 0:
+                pool = results if section < 2 else results_v
+                results_of[index] = pool.tile([P, GROUP_HEADS, t_run, DH], F32, name="result")
+            result = results_of[index]
+            acc = (psum_v if section < 2 else psum_s).tile([P, N_COLS], F32, tag="bank", name="acc")
+            for g in range(PASSES):
+                nc.tensor.matmul_mx(
+                    out=acc[:],
+                    lhsT=x_codes[:, t, g, :].bitcast(FP8X4),
+                    lhsT_scale=x_scales[:, t, g, :],
+                    rhs=w_codes[:, g, :].bitcast(FP8X4),
+                    rhs_scale=w_scales[:, g, :],
+                    start=(g == 0),
+                    stop=(g == PASSES - 1),
+                )
+            by_head = acc[:].rearrange("p (h d) -> p h d", h=GROUP_HEADS)
+            if section < 2:
+                if t % ADD_RUN == 0:
+                    products_of[index] = products.tile([P, ADD_RUN, 2, GROUP_HEADS, DH], F32, name="product")
+                product = products_of[index]
+                both = [P, 2, GROUP_HEADS, DH]
+                table = tables[section][:, t].rearrange("p e f i -> p e (f i)")
+                nc.vector.tensor_tensor(
+                    out=product[:, t % ADD_RUN],
+                    in0=by_head.unsqueeze(1).to_broadcast(both),
+                    in1=table.unsqueeze(2).to_broadcast(both),
+                    op=ALU.mult,
+                )
+                if t % ADD_RUN == ADD_RUN - 1:
+                    very_last = last_group and t == ROW_TILES - 1
+                    for adder, b0, b1 in ((nc.gpsimd, 0, 1), (nc.vector, 1, 2)) if very_last else ((nc.gpsimd, 0, 2),):
+                        terms = product[:, b0:b1].rearrange("p b e h d -> p (b e) h d")
+                        first = j + 1 - ADD_RUN
                         adder.tensor_tensor(
-                            out=result[:, :, :, lo : lo + HALF].rearrange("p h t d -> p t h d"),
-                            in0=product[:, :, 0, :, lo : lo + HALF],
-                            in1=product[:, :, 1, :, partner : partner + HALF],
+                            out=result[:, :, first + b0 : first + b1, :].rearrange("p h b (e i) -> p (b e) h i", e=2),
+                            in0=terms[:, :, :, 0:HALF],
+                            in1=terms[:, :, :, HALF:DH],
                             op=ALU.add,
                         )
+            else:
+                nc.scalar.copy(out=result[:, :, j, :], in_=by_head)
+            if j == t_run - 1:
                 store_queue = nc.sync if section < 2 else nc.scalar
-                store_queue.dma_start(
-                    out=out_view[:, first_head : first_head + GROUP_HEADS, t0 : t0 + t_run, :], in_=result[:]
-                )
+                out_view = outs[section][0].rearrange("h (p t) d -> p h t d", t=ROW_TILES)
+                heads = slice(half * GROUP_HEADS, (half + 1) * GROUP_HEADS)
+                store_queue.dma_start(out=out_view[:, heads, t - j : t + 1, :], in_=result[:])
+
+        row_scale(0)
+        sine_tables()
+        normalise(0)
+        turn(0)
+        row_scale(1)
+        regroup_weights(0)
+        normalise(1)
+        turn(1)
+        quantise_weights(0)
+        quantise_rows(0)
+        for t in range(1, ROW_TILES):
+            if t + 1 < ROW_TILES:
+                row_scale(t + 1)
+                normalise(t + 1)
+                turn(t + 1)
+            quantise_rows(t)
+            bank(0, t - 1)
+        regroup_weights(1)
+        quantise_weights(1)
+        bank(0, ROW_TILES - 1)
+        scaled_tables()
+        regroup_weights(2)
+        quantise_weights(2)
+        for t in range(ROW_TILES):
+            bank(1, t)
+        for rotary in (2, 4):
+            regroup_weights(rotary + 1)
+            quantise_weights(rotary + 1)
+            if rotary == 2:
+                regroup_weights(4)
+                quantise_weights(4)
+            for t in range(ROW_TILES):
+                bank(rotary, t)
+                bank(rotary + 1, t)

@@ -28,12 +28,10 @@ ROW_TILES = SEQ // P
 N_COLS = 512
 GROUP_HEADS = N_COLS // DH
 T_RUN = 4
-ADD_RUN = 2
+SPARE_EVERY = 4
 T_RUN_LAST = 2
 
-GROUPS = ((1, 0), (1, 1), (0, 0), (2, 0), (0, 1), (2, 1))
-
-LAST_ROTARY = 4
+GROUPS = ((1, 0), (1, 1), (2, 0), (0, 0), (2, 1), (0, 1))
 
 FLOPS = 2 * SEQ * DIM * 3 * HEADS * DH
 
@@ -44,11 +42,13 @@ def tile_ringattention_pa_kernel(tc, x, rotary_emb, gamma, w_qkv, out_q, out_k, 
     with ExitStack() as ctx:
         keep = ctx.enter_context(tc.tile_pool(name="keep", bufs=1))
         squares = ctx.enter_context(tc.tile_pool(name="squares", bufs=2))
-        normed = ctx.enter_context(tc.tile_pool(name="normed", bufs=3))
+        normed = ctx.enter_context(tc.tile_pool(name="normed", bufs=5))
+        x_words = ctx.enter_context(tc.tile_pool(name="x_words", bufs=3))
         w_in = ctx.enter_context(tc.tile_pool(name="w_in", bufs=len(GROUPS) - 1))
         w_words = ctx.enter_context(tc.tile_pool(name="w_words", bufs=3))
         w_mx = ctx.enter_context(tc.tile_pool(name="w_mx", bufs=4))
-        products = ctx.enter_context(tc.tile_pool(name="products", bufs=4))
+        products = ctx.enter_context(tc.tile_pool(name="products", bufs=6))
+        copies = ctx.enter_context(tc.tile_pool(name="copies", bufs=2))
         results = ctx.enter_context(tc.tile_pool(name="results", bufs=4))
         results_v = ctx.enter_context(tc.tile_pool(name="results_v", bufs=2))
         psum_v = ctx.enter_context(tc.psum_pool(name="psum_v", bufs=4))
@@ -75,8 +75,9 @@ def tile_ringattention_pa_kernel(tc, x, rotary_emb, gamma, w_qkv, out_q, out_k, 
 
         load_x(0)
         load_w(*GROUPS[0])
-        for t in range(2, ROW_TILES, 2):
-            load_x(t)
+        load_x(2)
+        load_x(4)
+        load_x(6)
         for section, half in GROUPS[1:]:
             load_w(section, half)
 
@@ -87,35 +88,32 @@ def tile_ringattention_pa_kernel(tc, x, rotary_emb, gamma, w_qkv, out_q, out_k, 
         minus_half = keep.tile([P, ROW_TILES], F32)
         nc.gpsimd.memset(minus_half[:], -0.5)
 
-        table_k = keep.tile([P, ROW_TILES, 2, 2, HALF], F32)
+        table = keep.tile([P, ROW_TILES, 2, 2, HALF], F32)
         table_q = keep.tile([P, ROW_TILES, 2, 2, HALF], F32)
         sin_half = keep.tile([P, ROW_TILES, DH], F32)
         nc.scalar.activation(out=sin_half[:], in_=angles[:], func=ACT.Sin, scale=0.5)
-        nc.vector.tensor_tensor(out=sin_half[:], in0=sin_half[:], in1=sin_half[:], op=ALU.mult)
-        for e in range(2):
+
+        def cosines():
+            nc.vector.tensor_tensor(out=sin_half[:], in0=sin_half[:], in1=sin_half[:], op=ALU.mult)
             nc.vector.tensor_scalar(
-                out=table_k[:, :, e, e, :], in0=sin_half[:, :, e * HALF : (e + 1) * HALF],
+                out=table[:].rearrange("p t e f i -> p t (e f) i")[:, :, 0:4:3, :],
+                in0=sin_half[:].rearrange("p t (e i) -> p t e i", e=2),
                 scalar1=-2.0, scalar2=1.0, op0=ALU.mult, op1=ALU.add,
             )
 
         def sine_tables():
-            nc.scalar.activation(out=table_k[:, :, 0, 1, :], in_=angles[:, :, 0:HALF], func=ACT.Sin, scale=-1.0)
-            nc.scalar.activation(out=table_k[:, :, 1, 0, :], in_=angles[:, :, HALF:DH], func=ACT.Sin)
+            nc.scalar.activation(out=table[:, :, 0, 1, :], in_=angles[:, :, 0:HALF], func=ACT.Sin, scale=-1.0)
+            nc.scalar.activation(out=table[:, :, 1, 0, :], in_=angles[:, :, HALF:DH], func=ACT.Sin)
 
-        def scaled_tables():
-            for e in range(2):
-                nc.gpsimd.tensor_scalar(
-                    out=table_q[:, :, e], in0=table_k[:, :, e], scalar1=math.sqrt(DH), scalar2=0.0,
-                    op0=ALU.mult, op1=ALU.add,
-                )
+        def scaled_table():
+            flat = "p t e f i -> p (t e f i)"
+            nc.vector.tensor_scalar_mul(out=table_q[:].rearrange(flat), in0=table[:].rearrange(flat), scalar1=math.sqrt(DH))
 
-        tables = (table_q, table_k)
-
-        gamma_all = []
+        gamma_all = psum_s.tile([P, DIM], BF16, tag="bank")
         for n in range(0, DIM, N_COLS):
-            spread = psum_s.tile([P, N_COLS], F32, tag="bank")
-            nc.tensor.matmul(out=spread[:], lhsT=ones[:], rhs=gamma_row[:, n : n + N_COLS], start=True, stop=True)
-            gamma_all.append(spread)
+            nc.tensor.matmul(
+                out=gamma_all[:, n : n + N_COLS], lhsT=ones[:], rhs=gamma_row[:, n : n + N_COLS], start=True, stop=True
+            )
 
         x_codes = keep.tile([P, ROW_TILES, PASSES, P], U32, align_bytes=64)
         x_scales = keep.tile([P, ROW_TILES, PASSES, P], U8, align_bytes=64)
@@ -123,32 +121,33 @@ def tile_ringattention_pa_kernel(tc, x, rotary_emb, gamma, w_qkv, out_q, out_k, 
         floored = keep.tile([P, ROW_TILES], F32)
         inv_rms = keep.tile([P, ROW_TILES], F32)
 
-        def row_scale(t):
+        def row_square(t):
             sq = squares.tile([P, DIM], BF16, name="sq")
             nc.scalar.activation(
                 out=sq[:], in_=x_rows[:, t, :], func=ACT.Square, scale=1.0 / math.sqrt(DIM),
                 accum_out=mean_sq[:, t : t + 1],
             )
+
+        def row_scale(t0, t1):
             nc.gpsimd.tensor_scalar(
-                out=floored[:, t : t + 1], in0=mean_sq[:, t : t + 1], scalar1=EPS * EPS / DIM, scalar2=None,
+                out=floored[:, t0:t1], in0=mean_sq[:, t0:t1], scalar1=EPS * EPS / DIM, scalar2=None,
                 op0=ALU.max,
             )
             nc.gpsimd.tensor_tensor(
-                out=inv_rms[:, t : t + 1], in0=floored[:, t : t + 1], in1=minus_half[:, t : t + 1], op=ALU.pow
+                out=inv_rms[:, t0:t1], in0=floored[:, t0:t1], in1=minus_half[:, t0:t1], op=ALU.pow
             )
 
         xn_of = {}
         words_of = {}
+        turned_of = {}
 
         def normalise(t):
             xn = normed.tile([P, DIM], BF16, name="xn")
             xn_of[t] = xn
-            for j, spread in enumerate(gamma_all):
-                cols = slice(j * N_COLS, (j + 1) * N_COLS)
-                nc.vector.scalar_tensor_tensor(
-                    out=xn[:, cols], in0=x_rows[:, t, cols], scalar=inv_rms[:, t : t + 1], in1=spread[:],
-                    op0=ALU.mult, op1=ALU.mult,
-                )
+            nc.vector.scalar_tensor_tensor(
+                out=xn[:], in0=x_rows[:, t, :], scalar=inv_rms[:, t : t + 1], in1=gamma_all[:],
+                op0=ALU.mult, op1=ALU.mult,
+            )
 
         def turn(t):
             pairs = xn_of[t][:].bitcast(F32)
@@ -157,9 +156,11 @@ def tile_ringattention_pa_kernel(tc, x, rotary_emb, gamma, w_qkv, out_q, out_k, 
                 for h in range(PAIRS):
                     first = g * P * PAIRS + h
                     nc.tensor.transpose(xn_t[:, g, h, :], pairs[:, first : (g + 1) * P * PAIRS : PAIRS], ident[:])
-            xn_words = normed.tile([P, PASSES, P, PAIRS], F32, align_bytes=64, name="xn_words")
-            nc.scalar.copy(out=xn_words[:], in_=xn_t[:].rearrange("p g h r -> p g r h"))
-            words_of[t] = xn_words
+            turned_of[t] = xn_t
+
+        def copy_out(t):
+            words_of[t] = x_words.tile([P, PASSES, P, PAIRS], F32, align_bytes=64, name="xn_words")
+            nc.scalar.copy(out=words_of[t][:], in_=turned_of[t][:].rearrange("p g h r -> p g r h"))
 
         def quantise_rows(t):
             nc.vector.quantize_mx(
@@ -171,14 +172,17 @@ def tile_ringattention_pa_kernel(tc, x, rotary_emb, gamma, w_qkv, out_q, out_k, 
         grouped_of = {}
         weights_of = {}
 
-        def regroup_weights(index):
-            grouped = w_words.tile([P, PASSES, N_COLS, PACK], BF16, align_bytes=64, name="grouped")
-            grouped_of[index] = grouped
+        def regroup_weights(index, pieces, of):
+            if 0 in pieces:
+                grouped_of[index] = w_words.tile([P, PASSES, N_COLS, PACK], BF16, align_bytes=64, name="grouped")
             regroup = nc.vector.tensor_copy if index == 0 else nc.scalar.copy
-            for g in range(PASSES):
+            width = PASSES * N_COLS // of
+            for piece in pieces:
+                g, first = divmod(piece * width, N_COLS)
+                cols = slice(first, first + width)
                 regroup(
-                    out=grouped[:, g].rearrange("p (c i) u -> p c u i", i=4),
-                    in_=w_raw[GROUPS[index]][:, g].rearrange("p u (c i) -> p c u i", i=4),
+                    out=grouped_of[index][:, g, cols].rearrange("p (c i) u -> p c u i", i=4),
+                    in_=w_raw[GROUPS[index]][:, g, :, cols].rearrange("p u (c i) -> p c u i", i=4),
                 )
 
         def quantise_weights(index):
@@ -192,19 +196,15 @@ def tile_ringattention_pa_kernel(tc, x, rotary_emb, gamma, w_qkv, out_q, out_k, 
             weights_of[index] = (codes, scales)
 
         results_of = {}
-        products_of = {}
+        acc_of = {}
 
-        def bank(index, t):
+        def by_scalar(index, t):
+            return GROUPS[index][0] == 2 or (index == 0 and t % SPARE_EVERY == 0)
+
+        def multiply(index, t):
             w_codes, w_scales = weights_of[index]
-            section, half = GROUPS[index]
-            last_group = index == LAST_ROTARY
-            t_run = T_RUN_LAST if last_group else T_RUN
-            j = t % t_run
-            if j == 0:
-                pool = results if section < 2 else results_v
-                results_of[index] = pool.tile([P, GROUP_HEADS, t_run, DH], F32, name="result")
-            result = results_of[index]
-            acc = (psum_v if section < 2 else psum_s).tile([P, N_COLS], F32, tag="bank", name="acc")
+            pool = psum_s if by_scalar(index, t) else psum_v
+            acc = pool.tile([P, N_COLS], F32, tag="bank", name="acc")
             for g in range(PASSES):
                 nc.tensor.matmul_mx(
                     out=acc[:],
@@ -215,30 +215,39 @@ def tile_ringattention_pa_kernel(tc, x, rotary_emb, gamma, w_qkv, out_q, out_k, 
                     start=(g == 0),
                     stop=(g == PASSES - 1),
                 )
+            acc_of[(index, t)] = acc
+
+        def finish(index, t):
+            section, half = GROUPS[index]
+            last_group = index == len(GROUPS) - 1
+            t_run = T_RUN_LAST if last_group else T_RUN
+            j = t % t_run
+            if j == 0:
+                pool = results if section < 2 else results_v
+                results_of[index] = pool.tile([P, GROUP_HEADS, t_run, DH], F32, name="result")
+            result = results_of[index]
+            acc = acc_of[(index, t)]
             by_head = acc[:].rearrange("p (h d) -> p h d", h=GROUP_HEADS)
             if section < 2:
-                if t % ADD_RUN == 0:
-                    products_of[index] = products.tile([P, ADD_RUN, 2, GROUP_HEADS, DH], F32, name="product")
-                product = products_of[index]
+                product = products.tile([P, 2, GROUP_HEADS, DH], F32, name="product")
                 both = [P, 2, GROUP_HEADS, DH]
-                table = tables[section][:, t].rearrange("p e f i -> p e (f i)")
-                nc.vector.tensor_tensor(
-                    out=product[:, t % ADD_RUN],
-                    in0=by_head.unsqueeze(1).to_broadcast(both),
-                    in1=table.unsqueeze(2).to_broadcast(both),
-                    op=ALU.mult,
+                angle_terms = (table_q if section == 0 else table)[:, t].rearrange("p e f i -> p e (f i)").unsqueeze(2).to_broadcast(both)
+                multiplier = nc.vector
+                if by_scalar(index, t):
+                    copied = copies.tile([P, N_COLS], F32, name="copied")
+                    nc.scalar.copy(out=copied[:], in_=acc[:])
+                    by_head = copied[:].rearrange("p (h d) -> p h d", h=GROUP_HEADS)
+                    multiplier = nc.gpsimd
+                multiplier.tensor_tensor(
+                    out=product[:], in0=by_head.unsqueeze(1).to_broadcast(both), in1=angle_terms, op=ALU.mult
                 )
-                if t % ADD_RUN == ADD_RUN - 1:
-                    very_last = last_group and t == ROW_TILES - 1
-                    for adder, b0, b1 in ((nc.gpsimd, 0, 1), (nc.vector, 1, 2)) if very_last else ((nc.gpsimd, 0, 2),):
-                        terms = product[:, b0:b1].rearrange("p b e h d -> p (b e) h d")
-                        first = j + 1 - ADD_RUN
-                        adder.tensor_tensor(
-                            out=result[:, :, first + b0 : first + b1, :].rearrange("p h b (e i) -> p (b e) h i", e=2),
-                            in0=terms[:, :, :, 0:HALF],
-                            in1=terms[:, :, :, HALF:DH],
-                            op=ALU.add,
-                        )
+                adder = nc.vector if last_group and t == ROW_TILES - 1 else nc.gpsimd
+                adder.tensor_tensor(
+                    out=result[:, :, j, :].rearrange("p h (e i) -> p e h i", e=2),
+                    in0=product[:, :, :, 0:HALF],
+                    in1=product[:, :, :, HALF:DH],
+                    op=ALU.add,
+                )
             else:
                 nc.scalar.copy(out=result[:, :, j, :], in_=by_head)
             if j == t_run - 1:
@@ -247,37 +256,92 @@ def tile_ringattention_pa_kernel(tc, x, rotary_emb, gamma, w_qkv, out_q, out_k, 
                 heads = slice(half * GROUP_HEADS, (half + 1) * GROUP_HEADS)
                 store_queue.dma_start(out=out_view[:, heads, t - j : t + 1, :], in_=result[:])
 
-        row_scale(0)
-        sine_tables()
-        normalise(0)
-        turn(0)
-        row_scale(1)
-        regroup_weights(0)
-        normalise(1)
-        turn(1)
-        quantise_weights(0)
-        quantise_rows(0)
-        for t in range(1, ROW_TILES):
-            if t + 1 < ROW_TILES:
-                row_scale(t + 1)
-                normalise(t + 1)
-                turn(t + 1)
-            quantise_rows(t)
-            bank(0, t - 1)
-        regroup_weights(1)
-        quantise_weights(1)
-        bank(0, ROW_TILES - 1)
-        scaled_tables()
-        regroup_weights(2)
-        quantise_weights(2)
-        for t in range(ROW_TILES):
-            bank(1, t)
-        for rotary in (2, 4):
-            regroup_weights(rotary + 1)
-            quantise_weights(rotary + 1)
-            if rotary == 2:
-                regroup_weights(4)
-                quantise_weights(4)
+        def bank(index, t):
+            multiply(index, t)
+            finish(index, t)
+
+        def prepare_row(t):
+            row_square(t)
+            row_scale(t, t + 1)
+
+        with tc.manual_schedule():
+            prepare_row(0)
+            cosines()
+            sine_tables()
+            prepare_row(1)
+            regroup_weights(0, (0,), 2)
+            normalise(0)
+            turn(0)
+            prepare_row(2)
+            regroup_weights(0, (1,), 2)
+            normalise(1)
+            turn(1)
+            prepare_row(3)
+            prepare_row(4)
+            quantise_weights(0)
+            normalise(2)
+            turn(2)
             for t in range(ROW_TILES):
-                bank(rotary, t)
-                bank(rotary + 1, t)
+                if t + 5 < ROW_TILES:
+                    prepare_row(t + 5)
+                copy_out(t)
+                if t + 3 < ROW_TILES:
+                    normalise(t + 3)
+                    turn(t + 3)
+                quantise_rows(t)
+                multiply(0, t)
+                if t >= 2:
+                    finish(0, t - 2)
+                if t in (4, 5):
+                    regroup_weights(1, (t - 4,), 2)
+            regroup_weights(2, (0, 1), 2)
+            quantise_weights(1)
+            multiply(1, 0)
+            multiply(1, 1)
+            finish(0, 6)
+            finish(0, 7)
+            regroup_weights(3, (0, 1), 2)
+            multiply(1, 2)
+            multiply(1, 3)
+            finish(1, 0)
+            quantise_weights(2)
+            for t in range(1, ROW_TILES):
+                finish(1, t)
+                if t + 3 < ROW_TILES:
+                    multiply(1, t + 3)
+                multiply(2, t - 1)
+                if t >= 2:
+                    finish(2, t - 2)
+                if t == 4:
+                    regroup_weights(5, (0,), 2)
+                if t == 5:
+                    quantise_weights(3)
+                if t == 6:
+                    regroup_weights(5, (1,), 2)
+                    scaled_table()
+            multiply(3, 0)
+            multiply(3, 1)
+            multiply(3, 2)
+            multiply(2, 7)
+            finish(2, 6)
+            finish(2, 7)
+            regroup_weights(4, (0, 1), 2)
+            for t in range(ROW_TILES):
+                if t + 3 < ROW_TILES:
+                    multiply(3, t + 3)
+                finish(3, t)
+                if t == 2:
+                    quantise_weights(5)
+                if t == 5:
+                    quantise_weights(4)
+                if t >= 6:
+                    multiply(4, t - 6)
+            for t in range(4):
+                multiply(5, t)
+            for t in range(ROW_TILES):
+                if t + 4 < ROW_TILES:
+                    multiply(5, t + 4)
+                if t + 2 < ROW_TILES:
+                    multiply(4, t + 2)
+                finish(5, t)
+                finish(4, t)

@@ -27,9 +27,9 @@ PAIRS = PACK // 2
 ROW_TILES = SEQ // P
 N_COLS = 512
 GROUP_HEADS = N_COLS // DH
-T_RUN = 4
 SPARE_EVERY = 4
-T_RUN_LAST = 2
+RUNS = (4, 4)
+RUNS_LAST = (4, 2, 2)
 
 GROUPS = ((1, 0), (1, 1), (2, 0), (0, 0), (2, 1), (0, 1))
 
@@ -107,7 +107,7 @@ def tile_ringattention_pa_kernel(tc, x, rotary_emb, gamma, w_qkv, out_q, out_k, 
 
         def scaled_table():
             flat = "p t e f i -> p (t e f i)"
-            nc.vector.tensor_scalar_mul(out=table_q[:].rearrange(flat), in0=table[:].rearrange(flat), scalar1=math.sqrt(DH))
+            nc.scalar.activation(out=table_q[:].rearrange(flat), in_=table[:].rearrange(flat), func=ACT.Copy, scale=math.sqrt(DH))
 
         gamma_all = psum_s.tile([P, DIM], BF16, tag="bank")
         for n in range(0, DIM, N_COLS):
@@ -220,8 +220,12 @@ def tile_ringattention_pa_kernel(tc, x, rotary_emb, gamma, w_qkv, out_q, out_k, 
         def finish(index, t):
             section, half = GROUPS[index]
             last_group = index == len(GROUPS) - 1
-            t_run = T_RUN_LAST if last_group else T_RUN
-            j = t % t_run
+            first = 0
+            for t_run in RUNS_LAST if last_group else RUNS:
+                if t < first + t_run:
+                    break
+                first += t_run
+            j = t - first
             if j == 0:
                 pool = results if section < 2 else results_v
                 results_of[index] = pool.tile([P, GROUP_HEADS, t_run, DH], F32, name="result")
@@ -254,7 +258,7 @@ def tile_ringattention_pa_kernel(tc, x, rotary_emb, gamma, w_qkv, out_q, out_k, 
                 store_queue = nc.sync if section < 2 else nc.scalar
                 out_view = outs[section][0].rearrange("h (p t) d -> p h t d", t=ROW_TILES)
                 heads = slice(half * GROUP_HEADS, (half + 1) * GROUP_HEADS)
-                store_queue.dma_start(out=out_view[:, heads, t - j : t + 1, :], in_=result[:])
+                store_queue.dma_start(out=out_view[:, heads, first : t + 1, :], in_=result[:])
 
         def bank(index, t):
             multiply(index, t)
@@ -312,36 +316,42 @@ def tile_ringattention_pa_kernel(tc, x, rotary_emb, gamma, w_qkv, out_q, out_k, 
                 multiply(2, t - 1)
                 if t >= 2:
                     finish(2, t - 2)
-                if t == 4:
-                    regroup_weights(5, (0,), 2)
-                if t == 5:
-                    quantise_weights(3)
-                if t == 6:
-                    regroup_weights(5, (1,), 2)
+                if t == 3:
                     scaled_table()
+                if t == 5:
+                    regroup_weights(4, (0,), 2)
+                    quantise_weights(3)
+                if t == 7:
+                    regroup_weights(4, (1,), 2)
             multiply(3, 0)
             multiply(3, 1)
             multiply(3, 2)
             multiply(2, 7)
             finish(2, 6)
             finish(2, 7)
-            regroup_weights(4, (0, 1), 2)
+            regroup_weights(5, (0,), 2)
             for t in range(ROW_TILES):
                 if t + 3 < ROW_TILES:
                     multiply(3, t + 3)
                 finish(3, t)
                 if t == 2:
-                    quantise_weights(5)
-                if t == 5:
                     quantise_weights(4)
-                if t >= 6:
-                    multiply(4, t - 6)
+                if t >= 3:
+                    multiply(4, t - 3)
+                if t >= 4:
+                    finish(4, t - 4)
+                if t == 4:
+                    regroup_weights(5, (1,), 2)
+                if t == 6:
+                    quantise_weights(5)
             for t in range(4):
                 multiply(5, t)
+            finish(4, 4)
             for t in range(ROW_TILES):
                 if t + 4 < ROW_TILES:
                     multiply(5, t + 4)
-                if t + 2 < ROW_TILES:
-                    multiply(4, t + 2)
+                if t < 3:
+                    multiply(4, t + 5)
                 finish(5, t)
-                finish(4, t)
+                if t < 3:
+                    finish(4, t + 5)

@@ -27,6 +27,7 @@ PAIRS = PACK // 2
 ROW_TILES = SEQ // P
 N_COLS = 512
 GROUP_HEADS = N_COLS // DH
+PRODUCT_RUN = 4
 SPARE_EVERY = 4
 RUNS = (4, 4)
 RUNS_LAST = (4, 2, 2)
@@ -42,14 +43,14 @@ def tile_ringattention_pa_kernel(tc, x, rotary_emb, gamma, w_qkv, out_q, out_k, 
     with ExitStack() as ctx:
         keep = ctx.enter_context(tc.tile_pool(name="keep", bufs=1))
         squares = ctx.enter_context(tc.tile_pool(name="squares", bufs=2))
-        normed = ctx.enter_context(tc.tile_pool(name="normed", bufs=5))
+        normed = ctx.enter_context(tc.tile_pool(name="normed", bufs=ROW_TILES))
         x_words = ctx.enter_context(tc.tile_pool(name="x_words", bufs=3))
-        w_in = ctx.enter_context(tc.tile_pool(name="w_in", bufs=len(GROUPS) - 1))
+        w_in = ctx.enter_context(tc.tile_pool(name="w_in", bufs=4))
         w_words = ctx.enter_context(tc.tile_pool(name="w_words", bufs=3))
         w_mx = ctx.enter_context(tc.tile_pool(name="w_mx", bufs=4))
-        products = ctx.enter_context(tc.tile_pool(name="products", bufs=6))
+        products = ctx.enter_context(tc.tile_pool(name="products", bufs=2))
         copies = ctx.enter_context(tc.tile_pool(name="copies", bufs=2))
-        results = ctx.enter_context(tc.tile_pool(name="results", bufs=4))
+        results = ctx.enter_context(tc.tile_pool(name="results", bufs=3))
         results_v = ctx.enter_context(tc.tile_pool(name="results_v", bufs=2))
         psum_v = ctx.enter_context(tc.psum_pool(name="psum_v", bufs=4))
         psum_s = ctx.enter_context(tc.psum_pool(name="psum_s", bufs=4))
@@ -197,6 +198,7 @@ def tile_ringattention_pa_kernel(tc, x, rotary_emb, gamma, w_qkv, out_q, out_k, 
 
         results_of = {}
         acc_of = {}
+        products_of = {}
 
         def by_scalar(index, t):
             return GROUPS[index][0] == 2 or (index == 0 and t % SPARE_EVERY == 0)
@@ -233,7 +235,9 @@ def tile_ringattention_pa_kernel(tc, x, rotary_emb, gamma, w_qkv, out_q, out_k, 
             acc = acc_of[(index, t)]
             by_head = acc[:].rearrange("p (h d) -> p h d", h=GROUP_HEADS)
             if section < 2:
-                product = products.tile([P, 2, GROUP_HEADS, DH], F32, name="product")
+                if t % PRODUCT_RUN == 0:
+                    products_of[index] = products.tile([P, PRODUCT_RUN, 2, GROUP_HEADS, DH], F32, name="product")
+                product = products_of[index][:, t % PRODUCT_RUN]
                 both = [P, 2, GROUP_HEADS, DH]
                 angle_terms = (table_q if section == 0 else table)[:, t].rearrange("p e f i -> p e (f i)").unsqueeze(2).to_broadcast(both)
                 multiplier = nc.vector
@@ -243,7 +247,7 @@ def tile_ringattention_pa_kernel(tc, x, rotary_emb, gamma, w_qkv, out_q, out_k, 
                     by_head = copied[:].rearrange("p (h d) -> p h d", h=GROUP_HEADS)
                     multiplier = nc.gpsimd
                 multiplier.tensor_tensor(
-                    out=product[:], in0=by_head.unsqueeze(1).to_broadcast(both), in1=angle_terms, op=ALU.mult
+                    out=product, in0=by_head.unsqueeze(1).to_broadcast(both), in1=angle_terms, op=ALU.mult
                 )
                 adder = nc.vector if last_group and t == ROW_TILES - 1 else nc.gpsimd
                 adder.tensor_tensor(

@@ -28,7 +28,7 @@ ROW_TILES = SEQ // P
 N_COLS = 512
 GROUP_HEADS = N_COLS // DH
 PRODUCT_RUN = 4
-SPARE_EVERY = 4
+SPARE_EVERY = 8
 RUNS = (4, 4)
 RUNS_LAST = (4, 2, 2)
 

@@ -30,7 +30,7 @@ GROUP_HEADS = N_COLS // DH
 PRODUCT_RUN = 4
 SPARE_EVERY = 8
 RUNS = (4, 4)
-RUNS_LAST = (4, 2, 2)
+RUNS_LAST = (4, 4)
 
 GROUPS = ((1, 0), (1, 1), (2, 0), (0, 0), (2, 1), (0, 1))
 
@@ -42,14 +42,14 @@ def tile_ringattention_pa_kernel(tc, x, rotary_emb, gamma, w_qkv, out_q, out_k, 
     outs = (out_q, out_k, out_v)
     with ExitStack() as ctx:
         keep = ctx.enter_context(tc.tile_pool(name="keep", bufs=1))
-        squares = ctx.enter_context(tc.tile_pool(name="squares", bufs=2))
+        squares = ctx.enter_context(tc.tile_pool(name="squares", bufs=1))
         normed = ctx.enter_context(tc.tile_pool(name="normed", bufs=ROW_TILES))
-        x_words = ctx.enter_context(tc.tile_pool(name="x_words", bufs=3))
+        x_words = ctx.enter_context(tc.tile_pool(name="x_words", bufs=2))
         w_in = ctx.enter_context(tc.tile_pool(name="w_in", bufs=4))
         w_words = ctx.enter_context(tc.tile_pool(name="w_words", bufs=3))
         w_mx = ctx.enter_context(tc.tile_pool(name="w_mx", bufs=4))
         products = ctx.enter_context(tc.tile_pool(name="products", bufs=2))
-        copies = ctx.enter_context(tc.tile_pool(name="copies", bufs=2))
+        copies = ctx.enter_context(tc.tile_pool(name="copies", bufs=1))
         results = ctx.enter_context(tc.tile_pool(name="results", bufs=3))
         results_v = ctx.enter_context(tc.tile_pool(name="results_v", bufs=2))
         psum_v = ctx.enter_context(tc.psum_pool(name="psum_v", bufs=4))
@@ -160,14 +160,17 @@ def tile_ringattention_pa_kernel(tc, x, rotary_emb, gamma, w_qkv, out_q, out_k, 
             turned_of[t] = xn_t
 
         def copy_out(t):
-            words_of[t] = x_words.tile([P, PASSES, P, PAIRS], F32, align_bytes=64, name="xn_words")
-            nc.scalar.copy(out=words_of[t][:], in_=turned_of[t][:].rearrange("p g h r -> p g r h"))
+            run, j = divmod(t, 2)
+            if j == 0:
+                words_of[run] = x_words.tile([P, 2, PASSES, P, PAIRS], F32, align_bytes=64, name="xn_words")
+            nc.scalar.copy(out=words_of[run][:, j], in_=turned_of[t][:].rearrange("p g h r -> p g r h"))
 
-        def quantise_rows(t):
+        def quantise_rows(t0, t1):
+            words = words_of[t0 // 2][:, t0 % 2 : t0 % 2 + t1 - t0]
             nc.vector.quantize_mx(
-                out=x_codes[:, t].rearrange("p g r -> p (g r)").bitcast(FP8X4),
-                scales=x_scales[:, t].rearrange("p g r -> p (g r)"),
-                in_=words_of[t][:].rearrange("p g r h -> p (g r h)").bitcast(BF16),
+                out=x_codes[:, t0:t1].rearrange("p t g r -> p (t g r)").bitcast(FP8X4),
+                scales=x_scales[:, t0:t1].rearrange("p t g r -> p (t g r)"),
+                in_=words.rearrange("p t g r h -> p (t g r h)").bitcast(BF16),
             )
 
         grouped_of = {}
@@ -296,8 +299,13 @@ def tile_ringattention_pa_kernel(tc, x, rotary_emb, gamma, w_qkv, out_q, out_k, 
                 if t + 3 < ROW_TILES:
                     normalise(t + 3)
                     turn(t + 3)
-                quantise_rows(t)
-                multiply(0, t)
+                if t < 2:
+                    quantise_rows(t, t + 1)
+                    multiply(0, t)
+                elif t % 2 == 1:
+                    quantise_rows(t - 1, t + 1)
+                    multiply(0, t - 1)
+                    multiply(0, t)
                 if t >= 2:
                     finish(0, t - 2)
                 if t in (4, 5):
@@ -344,7 +352,7 @@ def tile_ringattention_pa_kernel(tc, x, rotary_emb, gamma, w_qkv, out_q, out_k, 
                     multiply(4, t - 3)
                 if t >= 4:
                     finish(4, t - 4)
-                if t == 4:
+                if t == 3:
                     regroup_weights(5, (1,), 2)
                 if t == 6:
                     quantise_weights(5)

import math
from contextlib import ExitStack

import concourse.mybir as mybir
from concourse.masks import make_identity

FP8X4 = mybir.dt.float8_e4m3fn_x4
BF16 = mybir.dt.bfloat16
F32 = mybir.dt.float32
U32 = mybir.dt.uint32
U8 = mybir.dt.uint8
ACT = mybir.ActivationFunctionType
ALU = mybir.AluOpType

P = 128
SEQ = 1024
DIM = 1024
HEADS = 8
DH = 128
HALF = DH // 2
EPS = 1e-12

PACK = 4
K_PASS = P * PACK
PASSES = DIM // K_PASS
PAIRS = PACK // 2
ROW_TILES = SEQ // P
N_COLS = 512
GROUP_HEADS = N_COLS // DH
PRODUCT_RUN = 4
SPARE_EVERY = 8
RUNS = (4, 4)
RUNS_LAST = (4, 4)

GROUPS = ((1, 0), (1, 1), (2, 0), (0, 0), (2, 1), (0, 1))

FLOPS = 2 * SEQ * DIM * 3 * HEADS * DH


def tile_ringattention_pa_kernel(tc, x, rotary_emb, gamma, w_qkv, out_q, out_k, out_v):
    nc = tc.nc
    outs = (out_q, out_k, out_v)
    with ExitStack() as ctx:
        keep = ctx.enter_context(tc.tile_pool(name="keep", bufs=1))
        squares = ctx.enter_context(tc.tile_pool(name="squares", bufs=1))
        normed = ctx.enter_context(tc.tile_pool(name="normed", bufs=ROW_TILES))
        x_words = ctx.enter_context(tc.tile_pool(name="x_words", bufs=2))
        w_in = ctx.enter_context(tc.tile_pool(name="w_in", bufs=4))
        w_words = ctx.enter_context(tc.tile_pool(name="w_words", bufs=3))
        w_mx = ctx.enter_context(tc.tile_pool(name="w_mx", bufs=4))
        products = ctx.enter_context(tc.tile_pool(name="products", bufs=2))
        copies = ctx.enter_context(tc.tile_pool(name="copies", bufs=1))
        results = ctx.enter_context(tc.tile_pool(name="results", bufs=3))
        results_v = ctx.enter_context(tc.tile_pool(name="results_v", bufs=2))
        psum_v = ctx.enter_context(tc.psum_pool(name="psum_v", bufs=4))
        psum_s = ctx.enter_context(tc.psum_pool(name="psum_s", bufs=4))

        angles = keep.tile([P, ROW_TILES, DH], BF16)
        nc.sync.dma_start(out=angles[:], in_=rotary_emb.rearrange("(p t) d -> p t d", t=ROW_TILES))
        gamma_row = keep.tile([P, DIM], BF16)
        nc.vector.memset(gamma_row[:], 0.0)
        nc.sync.dma_start(out=gamma_row[0:1, :], in_=gamma.rearrange("(o k) -> o k", o=1))
        x_rows = keep.tile([P, ROW_TILES, DIM], BF16)
        x_view = x[0].rearrange("(p t) k -> p t k", t=ROW_TILES)
        w_view = w_qkv.rearrange("(g p u) n -> g p u n", p=P, u=PACK)
        w_raw = {}

        def load_x(t):
            nc.sync.dma_start(out=x_rows[:, t : t + 2, :], in_=x_view[:, t : t + 2, :])

        def load_w(section, half):
            first = (section * 2 + half) * N_COLS
            w_raw[(section, half)] = w_in.tile([P, PASSES, PACK, N_COLS], BF16, name="w_raw")
            for g in range(PASSES):
                nc.sync.dma_start(out=w_raw[(section, half)][:, g], in_=w_view[g, :, :, first : first + N_COLS])

        load_x(0)
        load_w(*GROUPS[0])
        load_x(2)
        load_x(4)
        load_x(6)
        for section, half in GROUPS[1:]:
            load_w(section, half)

        ident = keep.tile([P, P], F32)
        make_identity(nc, ident[:])
        ones = keep.tile([P, P], BF16)
        nc.vector.memset(ones[:], 1.0)
        minus_half = keep.tile([P, ROW_TILES], F32)
        nc.gpsimd.memset(minus_half[:], -0.5)

        table = keep.tile([P, ROW_TILES, 2, 2, HALF], F32)
        table_q = keep.tile([P, ROW_TILES, 2, 2, HALF], F32)
        sin_half = keep.tile([P, ROW_TILES, DH], F32)
        nc.scalar.activation(out=sin_half[:], in_=angles[:], func=ACT.Sin, scale=0.5)

        def cosines():
            nc.vector.tensor_tensor(out=sin_half[:], in0=sin_half[:], in1=sin_half[:], op=ALU.mult)
            nc.vector.tensor_scalar(
                out=table[:].rearrange("p t e f i -> p t (e f) i")[:, :, 0:4:3, :],
                in0=sin_half[:].rearrange("p t (e i) -> p t e i", e=2),
                scalar1=-2.0, scalar2=1.0, op0=ALU.mult, op1=ALU.add,
            )

        def sine_tables():
            nc.scalar.activation(out=table[:, :, 0, 1, :], in_=angles[:, :, 0:HALF], func=ACT.Sin, scale=-1.0)
            nc.scalar.activation(out=table[:, :, 1, 0, :], in_=angles[:, :, HALF:DH], func=ACT.Sin)

        def scaled_table():
            flat = "p t e f i -> p (t e f i)"
            nc.scalar.activation(out=table_q[:].rearrange(flat), in_=table[:].rearrange(flat), func=ACT.Copy, scale=math.sqrt(DH))

        gamma_all = psum_s.tile([P, DIM], BF16, tag="bank")
        for n in range(0, DIM, N_COLS):
            nc.tensor.matmul(
                out=gamma_all[:, n : n + N_COLS], lhsT=ones[:], rhs=gamma_row[:, n : n + N_COLS], start=True, stop=True
            )

        x_codes = keep.tile([P, ROW_TILES, PASSES, P], U32, align_bytes=64)
        x_scales = keep.tile([P, ROW_TILES, PASSES, P], U8, align_bytes=64)
        mean_sq = keep.tile([P, ROW_TILES], F32)
        floored = keep.tile([P, ROW_TILES], F32)
        inv_rms = keep.tile([P, ROW_TILES], F32)

        def row_square(t):
            sq = squares.tile([P, DIM], BF16, name="sq")
            nc.scalar.activation(
                out=sq[:], in_=x_rows[:, t, :], func=ACT.Square, scale=1.0 / math.sqrt(DIM),
                accum_out=mean_sq[:, t : t + 1],
            )

        def row_scale(t0, t1):
            nc.gpsimd.tensor_scalar(
                out=floored[:, t0:t1], in0=mean_sq[:, t0:t1], scalar1=EPS * EPS / DIM, scalar2=None,
                op0=ALU.max,
            )
            nc.gpsimd.tensor_tensor(
                out=inv_rms[:, t0:t1], in0=floored[:, t0:t1], in1=minus_half[:, t0:t1], op=ALU.pow
            )

        xn_of = {}
        words_of = {}
        turned_of = {}

        def normalise(t):
            xn = normed.tile([P, DIM], BF16, name="xn")
            xn_of[t] = xn
            nc.vector.scalar_tensor_tensor(
                out=xn[:], in0=x_rows[:, t, :], scalar=inv_rms[:, t : t + 1], in1=gamma_all[:],
                op0=ALU.mult, op1=ALU.mult,
            )

        def turn(t):
            pairs = xn_of[t][:].bitcast(F32)
            xn_t = psum_s.tile([P, PASSES, PAIRS, P], F32, tag="bank", name="xn_t")
            for g in range(PASSES):
                for h in range(PAIRS):
                    first = g * P * PAIRS + h
                    nc.tensor.transpose(xn_t[:, g, h, :], pairs[:, first : (g + 1) * P * PAIRS : PAIRS], ident[:])
            turned_of[t] = xn_t

        def copy_out(t):
            run, j = divmod(t, 2)
            if j == 0:
                words_of[run] = x_words.tile([P, 2, PASSES, P, PAIRS], F32, align_bytes=64, name="xn_words")
            nc.scalar.copy(out=words_of[run][:, j], in_=turned_of[t][:].rearrange("p g h r -> p g r h"))

        def quantise_rows(t0, t1):
            words = words_of[t0 // 2][:, t0 % 2 : t0 % 2 + t1 - t0]
            nc.vector.quantize_mx(
                out=x_codes[:, t0:t1].rearrange("p t g r -> p (t g r)").bitcast(FP8X4),
                scales=x_scales[:, t0:t1].rearrange("p t g r -> p (t g r)"),
                in_=words.rearrange("p t g r h -> p (t g r h)").bitcast(BF16),
            )

        grouped_of = {}
        weights_of = {}

        def regroup_weights(index, pieces, of):
            if 0 in pieces:
                grouped_of[index] = w_words.tile([P, PASSES, N_COLS, PACK], BF16, align_bytes=64, name="grouped")
            regroup = nc.vector.tensor_copy if index == 0 else nc.scalar.copy
            width = PASSES * N_COLS // of
            for piece in pieces:
                g, first = divmod(piece * width, N_COLS)
                cols = slice(first, first + width)
                regroup(
                    out=grouped_of[index][:, g, cols].rearrange("p (c i) u -> p c u i", i=4),
                    in_=w_raw[GROUPS[index]][:, g, :, cols].rearrange("p u (c i) -> p c u i", i=4),
                )

        def quantise_weights(index):
            codes = w_mx.tile([P, PASSES, N_COLS], U32, align_bytes=64, name="w_codes")
            scales = w_mx.tile([P, PASSES, N_COLS], U8, align_bytes=64, name="w_scales")
            nc.vector.quantize_mx(
                out=codes[:].rearrange("p g n -> p (g n)").bitcast(FP8X4),
                scales=scales[:].rearrange("p g n -> p (g n)"),
                in_=grouped_of[index][:].rearrange("p g n u -> p (g n u)"),
            )
            weights_of[index] = (codes, scales)

        results_of = {}
        acc_of = {}
        products_of = {}

        def by_scalar(index, t):
            return GROUPS[index][0] == 2 or (index == 0 and t % SPARE_EVERY == 0)

        def multiply(index, t):
            w_codes, w_scales = weights_of[index]
            pool = psum_s if by_scalar(index, t) else psum_v
            acc = pool.tile([P, N_COLS], F32, tag="bank", name="acc")
            for g in range(PASSES):
                nc.tensor.matmul_mx(
                    out=acc[:],
                    lhsT=x_codes[:, t, g, :].bitcast(FP8X4),
                    lhsT_scale=x_scales[:, t, g, :],
                    rhs=w_codes[:, g, :].bitcast(FP8X4),
                    rhs_scale=w_scales[:, g, :],
                    start=(g == 0),
                    stop=(g == PASSES - 1),
                )
            acc_of[(index, t)] = acc

        def finish(index, t):
            section, half = GROUPS[index]
            last_group = index == len(GROUPS) - 1
            first = 0
            for t_run in RUNS_LAST if last_group else RUNS:
                if t < first + t_run:
                    break
                first += t_run
            j = t - first
            if j == 0:
                pool = results if section < 2 else results_v
                results_of[index] = pool.tile([P, GROUP_HEADS, t_run, DH], F32, name="result")
            result = results_of[index]
            acc = acc_of[(index, t)]
            by_head = acc[:].rearrange("p (h d) -> p h d", h=GROUP_HEADS)
            if section < 2:
                if t % PRODUCT_RUN == 0:
                    products_of[index] = products.tile([P, PRODUCT_RUN, 2, GROUP_HEADS, DH], F32, name="product")
                product = products_of[index][:, t % PRODUCT_RUN]
                both = [P, 2, GROUP_HEADS, DH]
                angle_terms = (table_q if section == 0 else table)[:, t].rearrange("p e f i -> p e (f i)").unsqueeze(2).to_broadcast(both)
                multiplier = nc.vector
                if by_scalar(index, t):
                    copied = copies.tile([P, N_COLS], F32, name="copied")
                    nc.scalar.copy(out=copied[:], in_=acc[:])
                    by_head = copied[:].rearrange("p (h d) -> p h d", h=GROUP_HEADS)
                    multiplier = nc.gpsimd
                multiplier.tensor_tensor(
                    out=product, in0=by_head.unsqueeze(1).to_broadcast(both), in1=angle_terms, op=ALU.mult
                )
                adder = nc.vector if last_group and t == ROW_TILES - 1 else nc.gpsimd
                adder.tensor_tensor(
                    out=result[:, :, j, :].rearrange("p h (e i) -> p e h i", e=2),
                    in0=product[:, :, :, 0:HALF],
                    in1=product[:, :, :, HALF:DH],
                    op=ALU.add,
                )
            else:
                nc.scalar.copy(out=result[:, :, j, :], in_=by_head)
            if j == t_run - 1:
                store_queue = nc.sync if section < 2 else nc.scalar
                out_view = outs[section][0].rearrange("h (p t) d -> p h t d", t=ROW_TILES)
                heads = slice(half * GROUP_HEADS, (half + 1) * GROUP_HEADS)
                store_queue.dma_start(out=out_view[:, heads, first : t + 1, :], in_=result[:])

        def bank(index, t):
            multiply(index, t)
            finish(index, t)

        def prepare_row(t):
            row_square(t)
            row_scale(t, t + 1)

        with tc.manual_schedule():
            prepare_row(0)
            cosines()
            sine_tables()
            prepare_row(1)
            regroup_weights(0, (0,), 2)
            normalise(0)
            turn(0)
            prepare_row(2)
            regroup_weights(0, (1,), 2)
            normalise(1)
            turn(1)
            prepare_row(3)
            prepare_row(4)
            quantise_weights(0)
            normalise(2)
            turn(2)
            for t in range(ROW_TILES):
                if t + 5 < ROW_TILES:
                    prepare_row(t + 5)
                copy_out(t)
                if t + 3 < ROW_TILES:
                    normalise(t + 3)
                    turn(t + 3)
                if t < 2:
                    quantise_rows(t, t + 1)
                    multiply(0, t)
                elif t % 2 == 1:
                    quantise_rows(t - 1, t + 1)
                    multiply(0, t - 1)
                    multiply(0, t)
                if t >= 2:
                    finish(0, t - 2)
                if t in (4, 5):
                    regroup_weights(1, (t - 4,), 2)
            regroup_weights(2, (0, 1), 2)
            quantise_weights(1)
            multiply(1, 0)
            multiply(1, 1)
            finish(0, 6)
            finish(0, 7)
            regroup_weights(3, (0, 1), 2)
            multiply(1, 2)
            multiply(1, 3)
            finish(1, 0)
            quantise_weights(2)
            for t in range(1, ROW_TILES):
                finish(1, t)
                if t + 3 < ROW_TILES:
                    multiply(1, t + 3)
                multiply(2, t - 1)
                if t >= 2:
                    finish(2, t - 2)
                if t == 3:
                    scaled_table()
                if t == 5:
                    regroup_weights(4, (0,), 2)
                    quantise_weights(3)
                if t == 7:
                    regroup_weights(4, (1,), 2)
            multiply(3, 0)
            multiply(3, 1)
            multiply(3, 2)
            multiply(2, 7)
            finish(2, 6)
            finish(2, 7)
            regroup_weights(5, (0,), 2)
            for t in range(ROW_TILES):
                if t + 3 < ROW_TILES:
                    multiply(3, t + 3)
                finish(3, t)
                if t == 2:
                    quantise_weights(4)
                if t >= 3:
                    multiply(4, t - 3)
                if t >= 4:
                    finish(4, t - 4)
                if t == 3:
                    regroup_weights(5, (1,), 2)
                if t == 6:
                    quantise_weights(5)
            for t in range(4):
                multiply(5, t)
            finish(4, 4)
            for t in range(ROW_TILES):
                if t + 4 < ROW_TILES:
                    multiply(5, t + 4)
                if t < 3:
                    multiply(4, t + 5)
                finish(5, t)
                if t < 3:
                    finish(4, t + 5)
